import numpy as np
import ml_dtypes

BF16 = ml_dtypes.bfloat16


def bf(x):
    return np.asarray(x, np.float32).astype(BF16)


def f32(x):
    return np.asarray(x, np.float32)


def f64(x):
    return np.asarray(x).astype(np.float64)


def striped(idx):
    return np.tile(idx.reshape(-1, 16).T, (8, 1))


V, D, M, N = 512, 128, 512, 256


def setup_inputs():
    return {"table": bf(np.random.standard_normal((V, D)) / np.sqrt(D)), "w": bf(np.random.standard_normal((D, M)) / np.sqrt(D)), "b": f32(0.1 * np.random.standard_normal((M, 1))), "offs": striped(np.random.permutation(np.tile(np.arange(V), 2))[:N])}


def reference(table, w, b, offs):
    idx = offs[:16].T.reshape(-1)
    return np.sqrt(D) * (f64(w).T @ f64(table)[idx].T) + f64(b)

@@ -1,0 +1,51 @@
+import math
+
+import concourse.mybir as mybir
+from concourse.masks import make_identity
+
+V, D, M, N = 512, 128, 512, 256
+P = 128
+FLOPS = 2 * D * M * N
+
+BF16, F32, U16 = mybir.dt.bfloat16, mybir.dt.float32, mybir.dt.uint16
+
+
+def tile_tidaltransformer_kernel(tc, table, w, b, offs, out):
+    nc = tc.nc
+    scale = math.sqrt(D)
+    with (
+        tc.tile_pool(name="held", bufs=1) as held,
+        tc.tile_pool(name="rows", bufs=V // P) as rows_pool,
+        tc.tile_pool(name="logits", bufs=M // P) as logits_pool,
+        tc.psum_pool(name="flip", bufs=1) as flip_pool,
+        tc.psum_pool(name="acc", bufs=M // P) as acc_pool,
+    ):
+        offsets = held.tile([P, N // 16], U16, name="offsets")
+        nc.sync.dma_start(offsets[:], offs)
+
+        head = held.tile([D, M], BF16, name="head")
+        nc.scalar.dma_start(head[:], w)
+
+        bias = held.tile([P, M // P], F32, name="bias")
+        with nc.allow_non_contiguous_dma(reason="2 KiB of bias, one float to a partition and block"):
+            nc.gpsimd.dma_start(bias[:], b.rearrange("(c p) one -> p (c one)", p=P))
+
+        identity = held.tile([P, P], BF16, name="identity")
+        make_identity(nc, identity[:])
+
+        flipped = flip_pool.tile([D, V], BF16, name="flipped")
+        for a in range(V // P):
+            rows = rows_pool.tile([P, D], BF16, name="rows")
+            nc.sync.dma_start(rows[:], table[a * P : (a + 1) * P, :])
+            nc.tensor.transpose(flipped[:, a * P : (a + 1) * P], rows[:], identity[:])
+        words = held.tile([D, V], BF16, name="words")
+        nc.vector.tensor_copy(words[:], flipped[:])
+
+        for c in range(M // P):
+            acc = acc_pool.tile([P, N], F32, name="acc")
+            nc.tensor.matmul(acc[:], head[:, c * P : (c + 1) * P], words[:].indirect(offsets[:]))
+            logits = logits_pool.tile([P, N], F32, name="logits")
+            nc.vector.tensor_scalar(
+                logits[:], acc[:], scale, bias[:, c : c + 1], mybir.AluOpType.mult, mybir.AluOpType.add
+            )
+            nc.sync.dma_start(out[c * P : (c + 1) * P, :], logits[:])

@@ -13,13 +13,21 @@ BF16, F32, U16 = mybir.dt.bfloat16, mybir.dt.float32, mybir.dt.uint16
 def tile_tidaltransformer_kernel(tc, table, w, b, offs, out):
     nc = tc.nc
     scale = math.sqrt(D)
+    half_words = V // 2
     with (
         tc.tile_pool(name="held", bufs=1) as held,
-        tc.tile_pool(name="rows", bufs=V // P) as rows_pool,
         tc.tile_pool(name="logits", bufs=M // P) as logits_pool,
-        tc.psum_pool(name="flip", bufs=1) as flip_pool,
+        tc.psum_pool(name="flip", bufs=2) as flip_pool,
         tc.psum_pool(name="acc", bufs=M // P) as acc_pool,
     ):
+        identity = held.tile([P, P], BF16, name="identity")
+        make_identity(nc, identity[:])
+
+        rows = held.tile([P, V // P, D], BF16, name="rows")
+        for h, queue in enumerate((nc.sync, nc.scalar)):
+            nc_rows = table[h * half_words : (h + 1) * half_words, :].rearrange("(a p) d -> p a d", p=P)
+            queue.dma_start(rows[:, 2 * h : 2 * h + 2, :], nc_rows)
+
         offsets = held.tile([P, N // 16], U16, name="offsets")
         nc.sync.dma_start(offsets[:], offs)
 
@@ -28,24 +36,29 @@ def tile_tidaltransformer_kernel(tc, table, w, b, offs, out):
 
         bias = held.tile([P, M // P], F32, name="bias")
         with nc.allow_non_contiguous_dma(reason="2 KiB of bias, one float to a partition and block"):
-            nc.gpsimd.dma_start(bias[:], b.rearrange("(c p) one -> p (c one)", p=P))
+            nc.sync.dma_start(bias[:], b.rearrange("(c p) one -> p (c one)", p=P))
 
-        identity = held.tile([P, P], BF16, name="identity")
-        make_identity(nc, identity[:])
-
-        flipped = flip_pool.tile([D, V], BF16, name="flipped")
-        for a in range(V // P):
-            rows = rows_pool.tile([P, D], BF16, name="rows")
-            nc.sync.dma_start(rows[:], table[a * P : (a + 1) * P, :])
-            nc.tensor.transpose(flipped[:, a * P : (a + 1) * P], rows[:], identity[:])
         words = held.tile([D, V], BF16, name="words")
-        nc.vector.tensor_copy(words[:], flipped[:])
+        for h in range(2):
+            flipped = flip_pool.tile([D, half_words], BF16, name="flipped")
+            for a in range(2):
+                nc.tensor.transpose(flipped[:, a * P : (a + 1) * P], rows[:, 2 * h + a, :], identity[:])
+            if h == 0:
+                nc.vector.tensor_copy(words[:, :half_words], flipped[:])
+            else:
+                nc.scalar.copy(words[:, half_words:], flipped[:])
 
         for c in range(M // P):
             acc = acc_pool.tile([P, N], F32, name="acc")
             nc.tensor.matmul(acc[:], head[:, c * P : (c + 1) * P], words[:].indirect(offsets[:]))
             logits = logits_pool.tile([P, N], F32, name="logits")
-            nc.vector.tensor_scalar(
-                logits[:], acc[:], scale, bias[:, c : c + 1], mybir.AluOpType.mult, mybir.AluOpType.add
-            )
-            nc.sync.dma_start(out[c * P : (c + 1) * P, :], logits[:])
+            if c % 2 == 0:
+                nc.vector.tensor_scalar(
+                    logits[:], acc[:], scale, bias[:, c : c + 1], mybir.AluOpType.mult, mybir.AluOpType.add
+                )
+                nc.sync.dma_start(out[c * P : (c + 1) * P, :], logits[:])
+            else:
+                nc.scalar.activation(
+                    logits[:], acc[:], mybir.ActivationFunctionType.Identity, bias=bias[:, c : c + 1], scale=scale
+                )
+                nc.scalar.dma_start(out[c * P : (c + 1) * P, :], logits[:])

@@ -44,15 +44,15 @@ def tile_tidaltransformer_kernel(tc, table, w, b, offs, out):
             for a in range(2):
                 nc.tensor.transpose(flipped[:, a * P : (a + 1) * P], rows[:, 2 * h + a, :], identity[:])
             if h == 0:
-                nc.vector.tensor_copy(words[:, :half_words], flipped[:])
+                nc.scalar.copy(words[:, :half_words], flipped[:])
             else:
-                nc.scalar.copy(words[:, half_words:], flipped[:])
+                nc.vector.tensor_copy(words[:, half_words:], flipped[:])
 
         for c in range(M // P):
             acc = acc_pool.tile([P, N], F32, name="acc")
             nc.tensor.matmul(acc[:], head[:, c * P : (c + 1) * P], words[:].indirect(offsets[:]))
             logits = logits_pool.tile([P, N], F32, name="logits")
-            if c % 2 == 0:
+            if c % 2 == 1:
                 nc.vector.tensor_scalar(
                     logits[:], acc[:], scale, bias[:, c : c + 1], mybir.AluOpType.mult, mybir.AluOpType.add
                 )

@@ -24,15 +24,15 @@ def tile_tidaltransformer_kernel(tc, table, w, b, offs, out):
         make_identity(nc, identity[:])
 
         rows = held.tile([P, V // P, D], BF16, name="rows")
-        for h, queue in enumerate((nc.sync, nc.scalar)):
+        for h in range(2):
             nc_rows = table[h * half_words : (h + 1) * half_words, :].rearrange("(a p) d -> p a d", p=P)
-            queue.dma_start(rows[:, 2 * h : 2 * h + 2, :], nc_rows)
+            nc.sync.dma_start(rows[:, 2 * h : 2 * h + 2, :], nc_rows)
 
         offsets = held.tile([P, N // 16], U16, name="offsets")
         nc.sync.dma_start(offsets[:], offs)
 
         head = held.tile([D, M], BF16, name="head")
-        nc.scalar.dma_start(head[:], w)
+        nc.sync.dma_start(head[:], w)
 
         bias = held.tile([P, M // P], F32, name="bias")
         with nc.allow_non_contiguous_dma(reason="2 KiB of bias, one float to a partition and block"):

@@ -43,22 +43,13 @@ def tile_tidaltransformer_kernel(tc, table, w, b, offs, out):
             flipped = flip_pool.tile([D, half_words], BF16, name="flipped")
             for a in range(2):
                 nc.tensor.transpose(flipped[:, a * P : (a + 1) * P], rows[:, 2 * h + a, :], identity[:])
-            if h == 0:
-                nc.scalar.copy(words[:, :half_words], flipped[:])
-            else:
-                nc.vector.tensor_copy(words[:, half_words:], flipped[:])
+            nc.vector.tensor_copy(words[:, h * half_words : (h + 1) * half_words], flipped[:])
 
         for c in range(M // P):
             acc = acc_pool.tile([P, N], F32, name="acc")
             nc.tensor.matmul(acc[:], head[:, c * P : (c + 1) * P], words[:].indirect(offsets[:]))
             logits = logits_pool.tile([P, N], F32, name="logits")
-            if c % 2 == 1:
-                nc.vector.tensor_scalar(
-                    logits[:], acc[:], scale, bias[:, c : c + 1], mybir.AluOpType.mult, mybir.AluOpType.add
-                )
-                nc.sync.dma_start(out[c * P : (c + 1) * P, :], logits[:])
-            else:
-                nc.scalar.activation(
-                    logits[:], acc[:], mybir.ActivationFunctionType.Identity, bias=bias[:, c : c + 1], scale=scale
-                )
-                nc.scalar.dma_start(out[c * P : (c + 1) * P, :], logits[:])
+            nc.vector.tensor_scalar(
+                logits[:], acc[:], scale, bias[:, c : c + 1], mybir.AluOpType.mult, mybir.AluOpType.add
+            )
+            nc.sync.dma_start(out[c * P : (c + 1) * P, :], logits[:])

@@ -13,20 +13,18 @@ BF16, F32, U16 = mybir.dt.bfloat16, mybir.dt.float32, mybir.dt.uint16
 def tile_tidaltransformer_kernel(tc, table, w, b, offs, out):
     nc = tc.nc
     scale = math.sqrt(D)
-    half_words = V // 2
     with (
         tc.tile_pool(name="held", bufs=1) as held,
         tc.tile_pool(name="logits", bufs=M // P) as logits_pool,
-        tc.psum_pool(name="flip", bufs=2) as flip_pool,
+        tc.psum_pool(name="flip", bufs=V // P) as flip_pool,
         tc.psum_pool(name="acc", bufs=M // P) as acc_pool,
     ):
         identity = held.tile([P, P], BF16, name="identity")
         make_identity(nc, identity[:])
 
         rows = held.tile([P, V // P, D], BF16, name="rows")
-        for h in range(2):
-            nc_rows = table[h * half_words : (h + 1) * half_words, :].rearrange("(a p) d -> p a d", p=P)
-            nc.sync.dma_start(rows[:, 2 * h : 2 * h + 2, :], nc_rows)
+        for a in range(V // P):
+            nc.sync.dma_start(rows[:, a, :], table[a * P : (a + 1) * P, :])
 
         offsets = held.tile([P, N // 16], U16, name="offsets")
         nc.sync.dma_start(offsets[:], offs)
@@ -39,11 +37,10 @@ def tile_tidaltransformer_kernel(tc, table, w, b, offs, out):
             nc.sync.dma_start(bias[:], b.rearrange("(c p) one -> p (c one)", p=P))
 
         words = held.tile([D, V], BF16, name="words")
-        for h in range(2):
-            flipped = flip_pool.tile([D, half_words], BF16, name="flipped")
-            for a in range(2):
-                nc.tensor.transpose(flipped[:, a * P : (a + 1) * P], rows[:, 2 * h + a, :], identity[:])
-            nc.vector.tensor_copy(words[:, h * half_words : (h + 1) * half_words], flipped[:])
+        for a in range(V // P):
+            flipped = flip_pool.tile([D, P], BF16, name="flipped")
+            nc.tensor.transpose(flipped[:], rows[:, a, :], identity[:])
+            nc.vector.tensor_copy(words[:, a * P : (a + 1) * P], flipped[:])
 
         for c in range(M // P):
             acc = acc_pool.tile([P, N], F32, name="acc")

@@ -29,12 +29,13 @@ def tile_tidaltransformer_kernel(tc, table, w, b, offs, out):
         offsets = held.tile([P, N // 16], U16, name="offsets")
         nc.sync.dma_start(offsets[:], offs)
 
-        head = held.tile([D, M], BF16, name="head")
-        nc.sync.dma_start(head[:], w)
-
+        heads = [held.tile([D, P], BF16, name="head%d" % c) for c in range(M // P)]
         bias = held.tile([P, M // P], F32, name="bias")
+        nc.sync.dma_start(heads[0][:], w[:, :P])
         with nc.allow_non_contiguous_dma(reason="2 KiB of bias, one float to a partition and block"):
             nc.sync.dma_start(bias[:], b.rearrange("(c p) one -> p (c one)", p=P))
+        for c in range(1, M // P):
+            nc.sync.dma_start(heads[c][:], w[:, c * P : (c + 1) * P])
 
         words = held.tile([D, V], BF16, name="words")
         for a in range(V // P):
@@ -44,7 +45,7 @@ def tile_tidaltransformer_kernel(tc, table, w, b, offs, out):
 
         for c in range(M // P):
             acc = acc_pool.tile([P, N], F32, name="acc")
-            nc.tensor.matmul(acc[:], head[:, c * P : (c + 1) * P], words[:].indirect(offsets[:]))
+            nc.tensor.matmul(acc[:], heads[c][:], words[:].indirect(offsets[:]))
             logits = logits_pool.tile([P, N], F32, name="logits")
             nc.vector.tensor_scalar(
                 logits[:], acc[:], scale, bias[:, c : c + 1], mybir.AluOpType.mult, mybir.AluOpType.add

@@ -7,6 +7,7 @@ V, D, M, N = 512, 128, 512, 256
 P = 128
 FLOPS = 2 * D * M * N
 
+IDENTITY = mybir.ActivationFunctionType.Identity
 BF16, F32, U16 = mybir.dt.bfloat16, mybir.dt.float32, mybir.dt.uint16
 
 
@@ -21,6 +22,11 @@ def tile_tidaltransformer_kernel(tc, table, w, b, offs, out):
     ):
         identity = held.tile([P, P], BF16, name="identity")
         make_identity(nc, identity[:])
+
+        zero = held.tile([P, 1], F32, name="zero")
+        still_zero = held.tile([P, 1], F32, name="still_zero")
+        nc.vector.memset(zero[:], 0.0)
+        nc.scalar.activation(still_zero[:], zero[:], IDENTITY, bias=zero[:], scale=scale)
 
         rows = held.tile([P, V // P, D], BF16, name="rows")
         for a in range(V // P):
@@ -47,7 +53,10 @@ def tile_tidaltransformer_kernel(tc, table, w, b, offs, out):
             acc = acc_pool.tile([P, N], F32, name="acc")
             nc.tensor.matmul(acc[:], heads[c][:], words[:].indirect(offsets[:]))
             logits = logits_pool.tile([P, N], F32, name="logits")
-            nc.vector.tensor_scalar(
-                logits[:], acc[:], scale, bias[:, c : c + 1], mybir.AluOpType.mult, mybir.AluOpType.add
-            )
+            if c % 2 == 0:
+                nc.scalar.activation(logits[:], acc[:], IDENTITY, bias=bias[:, c : c + 1], scale=scale)
+            else:
+                nc.vector.tensor_scalar(
+                    logits[:], acc[:], scale, bias[:, c : c + 1], mybir.AluOpType.mult, mybir.AluOpType.add
+                )
             nc.sync.dma_start(out[c * P : (c + 1) * P, :], logits[:])

@@ -17,8 +17,7 @@ def tile_tidaltransformer_kernel(tc, table, w, b, offs, out):
     with (
         tc.tile_pool(name="held", bufs=1) as held,
         tc.tile_pool(name="logits", bufs=M // P) as logits_pool,
-        tc.psum_pool(name="flip", bufs=V // P) as flip_pool,
-        tc.psum_pool(name="acc", bufs=M // P) as acc_pool,
+        tc.psum_pool(name="psum", bufs=8) as psum,
     ):
         identity = held.tile([P, P], BF16, name="identity")
         make_identity(nc, identity[:])
@@ -45,18 +44,26 @@ def tile_tidaltransformer_kernel(tc, table, w, b, offs, out):
 
         words = held.tile([D, V], BF16, name="words")
         for a in range(V // P):
-            flipped = flip_pool.tile([D, P], BF16, name="flipped")
+            flipped = psum.tile([D, P], BF16, name="flipped", tag="bank")
             nc.tensor.transpose(flipped[:], rows[:, a, :], identity[:])
             nc.vector.tensor_copy(words[:, a * P : (a + 1) * P], flipped[:])
 
         for c in range(M // P):
-            acc = acc_pool.tile([P, N], F32, name="acc")
-            nc.tensor.matmul(acc[:], heads[c][:], words[:].indirect(offsets[:]))
             logits = logits_pool.tile([P, N], F32, name="logits")
-            if c % 2 == 0:
-                nc.scalar.activation(logits[:], acc[:], IDENTITY, bias=bias[:, c : c + 1], scale=scale)
-            else:
-                nc.vector.tensor_scalar(
-                    logits[:], acc[:], scale, bias[:, c : c + 1], mybir.AluOpType.mult, mybir.AluOpType.add
-                )
+            pieces = 2 if c == M // P - 1 else 1
+            width = N // pieces
+            for j in range(pieces):
+                tokens = slice(j * width, (j + 1) * width)
+                lists = slice(j * width // 16, (j + 1) * width // 16)
+                acc = psum.tile([P, width], F32, name="acc", tag="bank")
+                nc.tensor.matmul(acc[:], heads[c][:], words[:].indirect(offsets[:, lists]))
+                if c % 2 == 0:
+                    nc.scalar.activation(
+                        logits[:, tokens], acc[:], IDENTITY, bias=bias[:, c : c + 1], scale=scale
+                    )
+                else:
+                    nc.vector.tensor_scalar(
+                        logits[:, tokens], acc[:], scale, bias[:, c : c + 1],
+                        mybir.AluOpType.mult, mybir.AluOpType.add,
+                    )
             nc.sync.dma_start(out[c * P : (c + 1) * P, :], logits[:])

import math

import concourse.mybir as mybir
from concourse.masks import make_identity

V, D, M, N = 512, 128, 512, 256
P = 128
FLOPS = 2 * D * M * N

IDENTITY = mybir.ActivationFunctionType.Identity
BF16, F32, U16 = mybir.dt.bfloat16, mybir.dt.float32, mybir.dt.uint16


def tile_tidaltransformer_kernel(tc, table, w, b, offs, out):
    nc = tc.nc
    scale = math.sqrt(D)
    with (
        tc.tile_pool(name="held", bufs=1) as held,
        tc.tile_pool(name="logits", bufs=M // P) as logits_pool,
        tc.psum_pool(name="psum", bufs=8) as psum,
    ):
        identity = held.tile([P, P], BF16, name="identity")
        make_identity(nc, identity[:])

        zero = held.tile([P, 1], F32, name="zero")
        still_zero = held.tile([P, 1], F32, name="still_zero")
        nc.vector.memset(zero[:], 0.0)
        nc.scalar.activation(still_zero[:], zero[:], IDENTITY, bias=zero[:], scale=scale)

        rows = held.tile([P, V // P, D], BF16, name="rows")
        for a in range(V // P):
            nc.sync.dma_start(rows[:, a, :], table[a * P : (a + 1) * P, :])

        offsets = held.tile([P, N // 16], U16, name="offsets")
        nc.sync.dma_start(offsets[:], offs)

        heads = [held.tile([D, P], BF16, name="head%d" % c) for c in range(M // P)]
        bias = held.tile([P, M // P], F32, name="bias")
        nc.sync.dma_start(heads[0][:], w[:, :P])
        with nc.allow_non_contiguous_dma(reason="2 KiB of bias, one float to a partition and block"):
            nc.sync.dma_start(bias[:], b.rearrange("(c p) one -> p (c one)", p=P))
        for c in range(1, M // P):
            nc.sync.dma_start(heads[c][:], w[:, c * P : (c + 1) * P])

        words = held.tile([D, V], BF16, name="words")
        for a in range(V // P):
            flipped = psum.tile([D, P], BF16, name="flipped", tag="bank")
            nc.tensor.transpose(flipped[:], rows[:, a, :], identity[:])
            nc.vector.tensor_copy(words[:, a * P : (a + 1) * P], flipped[:])

        for c in range(M // P):
            logits = logits_pool.tile([P, N], F32, name="logits")
            pieces = 2 if c == M // P - 1 else 1
            width = N // pieces
            for j in range(pieces):
                tokens = slice(j * width, (j + 1) * width)
                lists = slice(j * width // 16, (j + 1) * width // 16)
                acc = psum.tile([P, width], F32, name="acc", tag="bank")
                nc.tensor.matmul(acc[:], heads[c][:], words[:].indirect(offsets[:, lists]))
                if c % 2 == 0:
                    nc.scalar.activation(
                        logits[:, tokens], acc[:], IDENTITY, bias=bias[:, c : c + 1], scale=scale
                    )
                else:
                    nc.vector.tensor_scalar(
                        logits[:, tokens], acc[:], scale, bias[:, c : c + 1],
                        mybir.AluOpType.mult, mybir.AluOpType.add,
                    )
            nc.sync.dma_start(out[c * P : (c + 1) * P, :], logits[:])
